import numpy as np
import ml_dtypes


def mxq(x, axis, fmt="e4m3"):
    dtype, down = {"e4m3": (ml_dtypes.float8_e4m3fn, 7), "e5m2": (ml_dtypes.float8_e5m2, 14)}[fmt]
    v = np.moveaxis(np.asarray(x, np.float32).astype(ml_dtypes.bfloat16).astype(np.float64), axis, -1)
    blocks = v.reshape(v.shape[:-1] + (-1, 32))
    amax = np.abs(blocks).max(-1, keepdims=True)
    byte = np.maximum(np.where(amax > 0, np.frexp(amax)[1] - 1 + 127, 0) - down, 1)
    scale = np.exp2(byte - 127.0)
    codes = (blocks / scale).astype(np.float32).astype(dtype).astype(np.float64)
    return np.moveaxis((codes * scale).reshape(v.shape), -1, axis)


WIDE = False


def mx_kscale(k):
    if not WIDE:
        return np.ones(k)
    levels = np.array([20, -20, 10, -10, 0])
    a = np.random.permutation(np.resize(levels, k // 512 * 4)).reshape(k // 512, 4)
    idx = np.arange(k)
    return np.exp2(a[idx // 512, idx % 128 // 32])


BF16 = ml_dtypes.bfloat16


def bf(x):
    return np.asarray(x, np.float32).astype(BF16)


def f64(x):
    return np.asarray(x).astype(np.float64)


B, IN_DIM, HID, ATT = 3072, 256, 512, 256
TOTAL = IN_DIM + HID + ATT


def softplus(v):
    return np.logaddexp(v, 0.0)


def sigmoid(v):
    return 1.0 / (1.0 + np.exp(-v))


def setup_inputs():
    u = np.array(mx_kscale(HID), np.float64)
    uu = np.concatenate([u, u])
    h_ltc = bf(np.random.standard_normal((B, HID)))
    x_t = bf(np.random.standard_normal((B, IN_DIM)))
    context = bf(np.random.standard_normal((B, ATT)))
    W0 = bf(np.random.uniform(-1.0, 1.0, (2 * HID, TOTAL)) * 3.0 / np.sqrt(TOTAL))
    b_gd = bf(np.random.uniform(-0.1, 0.1, (2 * HID,)))
    W_tau = bf(np.random.uniform(-1.0, 1.0, (HID, HID)) * 2.0 / np.sqrt(HID))
    b_tau = bf(np.random.uniform(-0.1, 0.1, (HID,)))
    gleak = bf(np.random.uniform(0.001, 1.0, (HID,)))
    cm = bf(np.random.uniform(0.4, 0.6, (HID,)))
    g = bf(np.random.standard_normal((B, HID)) * np.exp2(np.random.randint(-12, 1, (B, 1))) * 64.0 * u[None, :])
    combined = np.concatenate([f64(x_t), f64(h_ltc), f64(context)], axis=1)
    g_d = combined @ f64(W0).T + f64(b_gd)
    tau = softplus(f64(h_ltc) @ f64(W_tau).T + f64(b_tau))
    return {"t": 0.0,
            "h_ltc": h_ltc,
            "x_t": x_t,
            "context": context,
            "W_gd": bf(f64(W0) / uu[:, None]),
            "b_gd": b_gd,
            "W_tau": W_tau,
            "b_tau": b_tau,
            "gleak": gleak,
            "cm": cm,
            "g_d": np.asarray(g_d, np.float32),
            "tau": np.asarray(tau, np.float32),
            "grad_out": g}


def reference(t, h_ltc, x_t, context, W_gd, b_gd, W_tau, b_tau, gleak, cm, g_d, tau, grad_out):
    gd = f64(g_d)
    sg = sigmoid(gd[:, :HID])
    th = np.tanh(gd[:, HID:])
    r = 1.0 / (f64(tau) + softplus(f64(cm)) + softplus(f64(gleak)) + 1e-6)
    dn = f64(grad_out) * r
    d_gate = dn * th * sg * (1.0 - sg)
    d_dyn = dn * sg * (1.0 - th * th)
    d_gd = np.concatenate([d_gate, d_dyn], axis=1)
    w_x = f64(W_gd)[:, :IN_DIM]
    return mxq(d_gd, 1, "e5m2") @ mxq(w_x, 0, "e4m3")

@@ -1,0 +1,263 @@
+from contextlib import ExitStack
+
+import concourse.mybir as mybir
+from concourse.masks import make_identity
+
+F32 = mybir.dt.float32
+BF16 = mybir.dt.bfloat16
+U32 = mybir.dt.uint32
+U8 = mybir.dt.uint8
+E5M2_X4 = mybir.dt.float8_e5m2_x4
+E4M3_X4 = mybir.dt.float8_e4m3fn_x4
+ACT = mybir.ActivationFunctionType
+ALU = mybir.AluOpType
+
+P = 128
+TOKENS, HID, IN_DIM = 3072, 512, 256
+PACK = 4
+HALVES = 2
+TILES = TOKENS // P
+GROUP = 4
+GD_TILES = 2
+GD_BUFS = 4
+G_TILES = 8
+MOVING = 512
+
+FLOPS = 2 * TOKENS * HALVES * HID * IN_DIM
+BYTES = (
+    TOKENS * HALVES * HID * 4
+    + TOKENS * HID * 4
+    + TOKENS * HID * 2
+    + HALVES * HID * IN_DIM * 2
+    + 2 * HID * 2
+    + TOKENS * IN_DIM * 4
+)
+
+
+def tile_ltcattentioncell_t_v_kernel(
+    tc, t, h_ltc, x_t, context, W_gd, b_gd, W_tau, b_tau, gleak, cm, g_d, tau, grad_out, out
+):
+    nc = tc.nc
+    tau_rows = tau.rearrange("(p i) h -> p i h", i=TILES)
+    gd_rows = g_d.rearrange("(p i) k -> p i k", i=TILES)
+    grad_rows = grad_out.rearrange("(p i) h -> p i h", i=TILES)
+    out_rows = out.rearrange("(p i) n -> p i n", i=TILES)
+
+    with ExitStack() as ctx:
+        ctx.enter_context(tc.manual_schedule())
+        const = ctx.enter_context(tc.tile_pool(name="const", bufs=1))
+        tau_pool = ctx.enter_context(tc.tile_pool(name="tau", bufs=4))
+        gd_pool = ctx.enter_context(tc.tile_pool(name="gd", bufs=GD_BUFS))
+        work = ctx.enter_context(tc.tile_pool(name="work", bufs=3))
+        store = ctx.enter_context(tc.tile_pool(name="store", bufs=2))
+
+        ident_bf16 = const.tile([P, P], BF16)
+        make_identity(nc, ident_bf16[:])
+        ident_f32 = const.tile([P, P], F32)
+        make_identity(nc, ident_f32[:])
+
+        log_s = const.tile([P, PACK, TILES, P], F32)
+
+        with tc.psum_pool(name="psum_ln", bufs=7) as psum_ln:
+            vec_rows = const.tile([P, P], BF16)
+            nc.vector.memset(vec_rows[:], 0.0)
+            nc.sync.dma_start(out=vec_rows[0:PACK, :], in_=cm.rearrange("(t p) -> t p", p=P))
+            nc.sync.dma_start(
+                out=vec_rows[PACK : 2 * PACK, :], in_=gleak.rearrange("(t p) -> t p", p=P)
+            )
+            vec_cols = psum_ln.tile([P, P], BF16, bufs=1)
+            nc.tensor.transpose(vec_cols[:], vec_rows[:], ident_bf16[:])
+            v = const.tile([P, 2 * PACK], F32)
+            nc.vector.tensor_copy(out=v[:], in_=vec_cols[:, 0 : 2 * PACK])
+            one = const.tile([P, 1], F32)
+            nc.vector.memset(one[:], 1.0)
+            v_abs = const.tile([P, 2 * PACK], F32)
+            nc.scalar.activation(out=v_abs[:], in_=v[:], func=ACT.Abs)
+            v_exp = const.tile([P, 2 * PACK], F32)
+            nc.scalar.activation(out=v_exp[:], in_=v_abs[:], func=ACT.Exp, scale=-1.0)
+            v_log = const.tile([P, 2 * PACK], F32)
+            nc.scalar.activation(out=v_log[:], in_=v_exp[:], func=ACT.Ln, bias=one[:])
+            softplus = const.tile([P, 2 * PACK], F32)
+            nc.vector.scalar_tensor_tensor(
+                out=softplus[:], in0=v[:], scalar=0.0, in1=v_log[:], op0=ALU.max, op1=ALU.add
+            )
+            c = const.tile([P, PACK], F32)
+            nc.vector.scalar_tensor_tensor(
+                out=c[:],
+                in0=softplus[:, 0:PACK],
+                scalar=1e-6,
+                in1=softplus[:, PACK : 2 * PACK],
+                op0=ALU.add,
+                op1=ALU.add,
+            )
+
+            for q in range(TILES // GROUP):
+                tiles_q = slice(q * GROUP, (q + 1) * GROUP)
+                tau_sb = tau_pool.tile([P, GROUP, HID], F32)
+                nc.sync.dma_start(out=tau_sb[:], in_=tau_rows[:, tiles_q, :])
+                for chunk in range(PACK):
+                    tau_t = psum_ln.tile([P, GROUP, P], F32)
+                    for j in range(GROUP):
+                        nc.tensor.transpose(
+                            tau_t[:, j, :], tau_sb[:, j, chunk * P : (chunk + 1) * P], ident_f32[:]
+                        )
+                    nc.scalar.activation(
+                        out=log_s[:, chunk, tiles_q, :],
+                        in_=tau_t[:],
+                        func=ACT.Ln,
+                        bias=c[:, chunk : chunk + 1],
+                    )
+
+        psum = ctx.enter_context(tc.psum_pool(name="psum", bufs=2, reuse_waits="tile"))
+
+        w_view = W_gd.rearrange("(g t p) n -> g p t n", t=PACK, p=P)
+        w_raw = const.tile([P, HALVES, PACK, IN_DIM], BF16)
+        for half in range(HALVES):
+            nc.sync.dma_start(out=w_raw[:, half], in_=w_view[half, :, :, 0:IN_DIM])
+        w_grouped = const.tile([P, HALVES, IN_DIM, PACK], BF16, align_bytes=64)
+        for half in range(HALVES):
+            nc.vector.tensor_copy(
+                out=w_grouped[:, half], in_=w_raw[:, half].rearrange("p t n -> p n t")
+            )
+        w_codes = const.tile([P, 2 * HALVES * IN_DIM], U32, align_bytes=64)
+        w_scales = const.tile([P, 2 * HALVES * IN_DIM], U8, align_bytes=64)
+        for copy in range(2):
+            cols = slice(copy * HALVES * IN_DIM, (copy + 1) * HALVES * IN_DIM)
+            nc.vector.quantize_mx(
+                out=w_codes[:, cols].bitcast(E4M3_X4),
+                scales=w_scales[:, cols],
+                in_=w_grouped[:].rearrange("p g n t -> p (g n t)"),
+            )
+
+        grad_sb = const.tile([P, TILES, HID], BF16)
+        gd_sb = {}
+
+        def load_grad(first):
+            tiles = slice(first, first + G_TILES)
+            nc.sync.dma_start(out=grad_sb[:, tiles, :], in_=grad_rows[:, tiles, :])
+
+        def load_gd(k):
+            tiles = slice(k * GD_TILES, (k + 1) * GD_TILES)
+            gd_sb[k] = gd_pool.tile([P, GD_TILES, HALVES * HID], F32, name="gd_sb")
+            nc.sync.dma_start(out=gd_sb[k][:], in_=gd_rows[:, tiles, :])
+
+        load_grad(0)
+        load_gd(0)
+        load_gd(1)
+        load_grad(G_TILES)
+        load_gd(2)
+        load_gd(3)
+        load_grad(2 * G_TILES)
+
+        gate_t, dyn_t, grad_t, acc = {}, {}, {}, {}
+        recip, tg, th, th_sq, dn, m, d_gd, codes, scales, out_sb = {}, {}, {}, {}, {}, {}, {}, {}, {}, {}
+
+        def transpose_inputs(i):
+            rows = gd_sb[i // GD_TILES][:, i % GD_TILES, :]
+            gate_t[i] = psum.tile([P, PACK, P], F32, name="gate_t")
+            dyn_t[i] = psum.tile([P, PACK, P], F32, name="dyn_t")
+            grad_t[i] = psum.tile([P, PACK, P], BF16, name="grad_t")
+            for chunk in range(PACK):
+                cols = slice(chunk * P, (chunk + 1) * P)
+                nc.tensor.transpose(gate_t[i][:, chunk, :], rows[:, cols], ident_f32[:])
+            for chunk in range(PACK):
+                cols = slice(HID + chunk * P, HID + (chunk + 1) * P)
+                nc.tensor.transpose(dyn_t[i][:, chunk, :], rows[:, cols], ident_f32[:])
+            for chunk in range(PACK):
+                cols = slice(chunk * P, (chunk + 1) * P)
+                nc.tensor.transpose(grad_t[i][:, chunk, :], grad_sb[:, i, cols], ident_bf16[:])
+            if i % GD_TILES == GD_TILES - 1 and (i // GD_TILES + GD_BUFS) * GD_TILES < TILES:
+                load_gd(i // GD_TILES + GD_BUFS)
+
+        def reciprocal(i):
+            recip[i] = work.tile([P, PACK, P], F32, name="recip")
+            nc.scalar.activation(out=recip[i][:], in_=log_s[:, :, i, :], func=ACT.Exp, scale=-1.0)
+
+        def activations(i):
+            tg[i] = work.tile([P, P, PACK], F32, name="tg")
+            th[i] = work.tile([P, P, PACK], F32, name="th")
+            th_sq[i] = work.tile([P, P, PACK], F32, name="th_sq")
+            nc.scalar.activation(
+                out=tg[i][:], in_=gate_t[i][:].rearrange("p t w -> p w t"), func=ACT.Tanh, scale=0.5
+            )
+            nc.scalar.activation(
+                out=th[i][:], in_=dyn_t[i][:].rearrange("p t w -> p w t"), func=ACT.Tanh
+            )
+            nc.scalar.activation(out=th_sq[i][:], in_=th[i][:], func=ACT.Square)
+
+        def scaled_gradient(i):
+            dn[i] = work.tile([P, P, PACK], F32, name="dn")
+            nc.vector.scalar_tensor_tensor(
+                out=dn[i][:],
+                in0=grad_t[i][:].rearrange("p t w -> p w t"),
+                scalar=-0.5,
+                in1=recip[i][:].rearrange("p t w -> p w t"),
+                op0=ALU.mult,
+                op1=ALU.mult,
+            )
+
+        def shared_factor(i):
+            m[i] = work.tile([P, P, PACK], F32, name="m")
+            nc.vector.scalar_tensor_tensor(
+                out=m[i][:], in0=tg[i][:], scalar=1.0, in1=dn[i][:], op0=ALU.add, op1=ALU.mult
+            )
+
+        def gradients(i):
+            d_gd[i] = work.tile([P, HALVES, P, PACK], BF16, name="d_gd", align_bytes=64)
+            gate_part = work.tile([P, P, PACK], F32, name="gate_part")
+            nc.vector.scalar_tensor_tensor(
+                out=gate_part[:], in0=tg[i][:], scalar=1.0, in1=m[i][:], op0=ALU.subtract, op1=ALU.mult
+            )
+            nc.vector.scalar_tensor_tensor(
+                out=d_gd[i][:, 1], in0=th_sq[i][:], scalar=1.0, in1=m[i][:], op0=ALU.subtract, op1=ALU.mult
+            )
+            nc.vector.scalar_tensor_tensor(
+                out=d_gd[i][:, 0], in0=gate_part[:], scalar=0.5, in1=th[i][:], op0=ALU.mult, op1=ALU.mult
+            )
+
+        def quantise(i):
+            codes[i] = work.tile([P, HALVES * P], U32, name="codes", align_bytes=64)
+            scales[i] = work.tile([P, HALVES * P], U8, name="scales", align_bytes=64)
+            nc.vector.quantize_mx(
+                out=codes[i][:].bitcast(E5M2_X4),
+                scales=scales[i][:],
+                in_=d_gd[i][:].rearrange("p g w t -> p (g w t)"),
+            )
+
+        def multiply(i):
+            acc[i] = psum.tile([P, MOVING], F32, name="acc")
+            for half in range(HALVES):
+                tokens = slice(half * P, (half + 1) * P)
+                w_cols = slice(half * IN_DIM, half * IN_DIM + MOVING)
+                nc.tensor.matmul_mx(
+                    out=acc[i][:],
+                    lhsT=codes[i][:, tokens].bitcast(E5M2_X4),
+                    lhsT_scale=scales[i][:, tokens],
+                    rhs=w_codes[:, w_cols].bitcast(E4M3_X4),
+                    rhs_scale=w_scales[:, w_cols],
+                    start=(half == 0),
+                    stop=(half == HALVES - 1),
+                )
+
+        def write_out(i):
+            q, j = divmod(i, GROUP)
+            if j == 0:
+                out_sb[q] = store.tile([P, GROUP, IN_DIM], F32, name="out_sb")
+            nc.scalar.copy(out=out_sb[q][:, j, :], in_=acc[i][:, 0:IN_DIM])
+            if j == GROUP - 1:
+                nc.sync.dma_start(out=out_rows[:, q * GROUP : (q + 1) * GROUP, :], in_=out_sb[q][:])
+
+        def run(stage, i):
+            if 0 <= i < TILES:
+                stage(i)
+
+        for n in range(-2, TILES + 2):
+            run(transpose_inputs, n + 2)
+            run(activations, n + 1)
+            run(reciprocal, n + 2)
+            run(shared_factor, n)
+            run(quantise, n - 1)
+            run(multiply, n - 1)
+            run(scaled_gradient, n + 1)
+            run(gradients, n)
+            run(write_out, n - 2)

@@ -178,10 +178,10 @@ def tile_ltcattentioncell_t_v_kernel(
             th[i] = work.tile([P, P, PACK], F32, name="th")
             th_sq[i] = work.tile([P, P, PACK], F32, name="th_sq")
             nc.scalar.activation(
-                out=tg[i][:], in_=gate_t[i][:].rearrange("p t w -> p w t"), func=ACT.Tanh, scale=0.5
+                out=th[i][:], in_=dyn_t[i][:].rearrange("p t w -> p w t"), func=ACT.Tanh
             )
             nc.scalar.activation(
-                out=th[i][:], in_=dyn_t[i][:].rearrange("p t w -> p w t"), func=ACT.Tanh
+                out=tg[i][:], in_=gate_t[i][:].rearrange("p t w -> p w t"), func=ACT.Tanh, scale=0.5
             )
             nc.scalar.activation(out=th_sq[i][:], in_=th[i][:], func=ACT.Square)
 

@@ -18,9 +18,12 @@ PACK = 4
 HALVES = 2
 TILES = TOKENS // P
 GROUP = 4
+BATCH_GROUPS = 3
+BATCH = BATCH_GROUPS * GROUP
+BATCHES = TILES // BATCH
+LEAD = 1 + (BATCHES - 1) * BATCH_GROUPS
 GD_TILES = 2
 GD_BUFS = 4
-G_TILES = 8
 MOVING = 512
 
 FLOPS = 2 * TOKENS * HALVES * HID * IN_DIM
@@ -46,74 +49,95 @@ def tile_ltcattentioncell_t_v_kernel(
     with ExitStack() as ctx:
         ctx.enter_context(tc.manual_schedule())
         const = ctx.enter_context(tc.tile_pool(name="const", bufs=1))
-        tau_pool = ctx.enter_context(tc.tile_pool(name="tau", bufs=4))
+        tau_pool = ctx.enter_context(tc.tile_pool(name="tau", bufs=BATCH_GROUPS))
         gd_pool = ctx.enter_context(tc.tile_pool(name="gd", bufs=GD_BUFS))
+        ahead = ctx.enter_context(tc.tile_pool(name="ahead", bufs=LEAD + 1))
         work = ctx.enter_context(tc.tile_pool(name="work", bufs=3))
-        store = ctx.enter_context(tc.tile_pool(name="store", bufs=2))
+        store = ctx.enter_context(tc.tile_pool(name="store", bufs=4))
+        psum = ctx.enter_context(tc.psum_pool(name="psum", bufs=2))
 
         ident_bf16 = const.tile([P, P], BF16)
         make_identity(nc, ident_bf16[:])
         ident_f32 = const.tile([P, P], F32)
         make_identity(nc, ident_f32[:])
 
-        log_s = const.tile([P, PACK, TILES, P], F32)
+        vec_rows = const.tile([P, P], BF16)
+        nc.vector.memset(vec_rows[:], 0.0)
+        nc.sync.dma_start(out=vec_rows[0:PACK, :], in_=cm.rearrange("(t p) -> t p", p=P))
+        nc.sync.dma_start(out=vec_rows[PACK : 2 * PACK, :], in_=gleak.rearrange("(t p) -> t p", p=P))
+        vec_cols = psum.tile([P, P], BF16, tag="grad_t")
+        nc.tensor.transpose(vec_cols[:], vec_rows[:], ident_bf16[:])
+        v = const.tile([P, 2 * PACK], F32)
+        nc.vector.tensor_copy(out=v[:], in_=vec_cols[:, 0 : 2 * PACK])
+        one = const.tile([P, 1], F32)
+        nc.vector.memset(one[:], 1.0)
+        v_abs = const.tile([P, 2 * PACK], F32)
+        nc.scalar.activation(out=v_abs[:], in_=v[:], func=ACT.Abs)
+        v_exp = const.tile([P, 2 * PACK], F32)
+        nc.scalar.activation(out=v_exp[:], in_=v_abs[:], func=ACT.Exp, scale=-1.0)
+        v_log = const.tile([P, 2 * PACK], F32)
+        nc.scalar.activation(out=v_log[:], in_=v_exp[:], func=ACT.Ln, bias=one[:])
+        softplus = const.tile([P, 2 * PACK], F32)
+        nc.vector.scalar_tensor_tensor(
+            out=softplus[:], in0=v[:], scalar=0.0, in1=v_log[:], op0=ALU.max, op1=ALU.add
+        )
+        c = const.tile([P, PACK], F32)
+        nc.vector.scalar_tensor_tensor(
+            out=c[:],
+            in0=softplus[:, 0:PACK],
+            scalar=1e-6,
+            in1=softplus[:, PACK : 2 * PACK],
+            op0=ALU.add,
+            op1=ALU.add,
+        )
 
-        with tc.psum_pool(name="psum_ln", bufs=7) as psum_ln:
-            vec_rows = const.tile([P, P], BF16)
-            nc.vector.memset(vec_rows[:], 0.0)
-            nc.sync.dma_start(out=vec_rows[0:PACK, :], in_=cm.rearrange("(t p) -> t p", p=P))
-            nc.sync.dma_start(
-                out=vec_rows[PACK : 2 * PACK, :], in_=gleak.rearrange("(t p) -> t p", p=P)
-            )
-            vec_cols = psum_ln.tile([P, P], BF16, bufs=1)
-            nc.tensor.transpose(vec_cols[:], vec_rows[:], ident_bf16[:])
-            v = const.tile([P, 2 * PACK], F32)
-            nc.vector.tensor_copy(out=v[:], in_=vec_cols[:, 0 : 2 * PACK])
-            one = const.tile([P, 1], F32)
-            nc.vector.memset(one[:], 1.0)
-            v_abs = const.tile([P, 2 * PACK], F32)
-            nc.scalar.activation(out=v_abs[:], in_=v[:], func=ACT.Abs)
-            v_exp = const.tile([P, 2 * PACK], F32)
-            nc.scalar.activation(out=v_exp[:], in_=v_abs[:], func=ACT.Exp, scale=-1.0)
-            v_log = const.tile([P, 2 * PACK], F32)
-            nc.scalar.activation(out=v_log[:], in_=v_exp[:], func=ACT.Ln, bias=one[:])
-            softplus = const.tile([P, 2 * PACK], F32)
-            nc.vector.scalar_tensor_tensor(
-                out=softplus[:], in0=v[:], scalar=0.0, in1=v_log[:], op0=ALU.max, op1=ALU.add
-            )
-            c = const.tile([P, PACK], F32)
-            nc.vector.scalar_tensor_tensor(
-                out=c[:],
-                in0=softplus[:, 0:PACK],
-                scalar=1e-6,
-                in1=softplus[:, PACK : 2 * PACK],
-                op0=ALU.add,
-                op1=ALU.add,
-            )
+        tau_sb, gd_sb = {}, {}
+        grad_sb = const.tile([P, TILES, HID], BF16)
 
-            for q in range(TILES // GROUP):
-                tiles_q = slice(q * GROUP, (q + 1) * GROUP)
-                tau_sb = tau_pool.tile([P, GROUP, HID], F32)
-                nc.sync.dma_start(out=tau_sb[:], in_=tau_rows[:, tiles_q, :])
-                for chunk in range(PACK):
-                    tau_t = psum_ln.tile([P, GROUP, P], F32)
-                    for j in range(GROUP):
-                        nc.tensor.transpose(
-                            tau_t[:, j, :], tau_sb[:, j, chunk * P : (chunk + 1) * P], ident_f32[:]
-                        )
-                    nc.scalar.activation(
-                        out=log_s[:, chunk, tiles_q, :],
-                        in_=tau_t[:],
-                        func=ACT.Ln,
-                        bias=c[:, chunk : chunk + 1],
+        def load_tau(q):
+            tau_sb[q] = tau_pool.tile([P, GROUP, HID], F32, name="tau_sb")
+            nc.sync.dma_start(out=tau_sb[q][:], in_=tau_rows[:, q * GROUP : (q + 1) * GROUP, :])
+
+        def load_grad(q):
+            tiles = slice(q * GROUP, (q + 1) * GROUP)
+            nc.sync.dma_start(out=grad_sb[:, tiles, :], in_=grad_rows[:, tiles, :])
+
+        def load_gd(k):
+            gd_sb[k] = gd_pool.tile([P, GD_TILES, HALVES * HID], F32, name="gd_sb")
+            nc.sync.dma_start(out=gd_sb[k][:], in_=gd_rows[:, k * GD_TILES : (k + 1) * GD_TILES, :])
+
+        log_s = const.tile([P, PACK, BATCH, P], F32)
+
+        def logarithms(q):
+            first = (q % BATCH_GROUPS) * GROUP
+            for chunk in range(PACK):
+                tau_t = psum.tile([P, GROUP, P], F32, tag=("gate_t", "dyn_t")[chunk % 2])
+                for j in range(GROUP):
+                    nc.tensor.transpose(
+                        tau_t[:, j, :], tau_sb[q][:, j, chunk * P : (chunk + 1) * P], ident_f32[:]
                     )
-
-        psum = ctx.enter_context(tc.psum_pool(name="psum", bufs=2, reuse_waits="tile"))
+                nc.scalar.activation(
+                    out=log_s[:, chunk, first : first + GROUP, :],
+                    in_=tau_t[:],
+                    func=ACT.Ln,
+                    bias=c[:, chunk : chunk + 1],
+                )
 
         w_view = W_gd.rearrange("(g t p) n -> g p t n", t=PACK, p=P)
         w_raw = const.tile([P, HALVES, PACK, IN_DIM], BF16)
+        load_tau(0)
         for half in range(HALVES):
             nc.sync.dma_start(out=w_raw[:, half], in_=w_view[half, :, :, 0:IN_DIM])
+        for q in range(1, BATCH_GROUPS):
+            load_tau(q)
+        load_grad(0)
+        for k in range(GD_BUFS):
+            load_gd(k)
+        load_grad(1)
+
+        for q in range(BATCH_GROUPS):
+            logarithms(q)
+
         w_grouped = const.tile([P, HALVES, IN_DIM, PACK], BF16, align_bytes=64)
         for half in range(HALVES):
             nc.vector.tensor_copy(
@@ -129,61 +153,45 @@ def tile_ltcattentioncell_t_v_kernel(
                 in_=w_grouped[:].rearrange("p g n t -> p (g n t)"),
             )
 
-        grad_sb = const.tile([P, TILES, HID], BF16)
-        gd_sb = {}
+        grad_t, acc = {}, {}
+        recip, tg, th, th_sq, dn, m, gate_part, d_gd, codes, scales = {}, {}, {}, {}, {}, {}, {}, {}, {}, {}
 
-        def load_grad(first):
-            tiles = slice(first, first + G_TILES)
-            nc.sync.dma_start(out=grad_sb[:, tiles, :], in_=grad_rows[:, tiles, :])
-
-        def load_gd(k):
-            tiles = slice(k * GD_TILES, (k + 1) * GD_TILES)
-            gd_sb[k] = gd_pool.tile([P, GD_TILES, HALVES * HID], F32, name="gd_sb")
-            nc.sync.dma_start(out=gd_sb[k][:], in_=gd_rows[:, tiles, :])
-
-        load_grad(0)
-        load_gd(0)
-        load_gd(1)
-        load_grad(G_TILES)
-        load_gd(2)
-        load_gd(3)
-        load_grad(2 * G_TILES)
-
-        gate_t, dyn_t, grad_t, acc = {}, {}, {}, {}
-        recip, tg, th, th_sq, dn, m, d_gd, codes, scales, out_sb = {}, {}, {}, {}, {}, {}, {}, {}, {}, {}
-
-        def transpose_inputs(i):
+        def activations(i):
             rows = gd_sb[i // GD_TILES][:, i % GD_TILES, :]
-            gate_t[i] = psum.tile([P, PACK, P], F32, name="gate_t")
-            dyn_t[i] = psum.tile([P, PACK, P], F32, name="dyn_t")
+            gate_t = psum.tile([P, PACK, P], F32)
+            dyn_t = psum.tile([P, PACK, P], F32)
+            for chunk in range(PACK):
+                cols = slice(chunk * P, (chunk + 1) * P)
+                nc.tensor.transpose(gate_t[:, chunk, :], rows[:, cols], ident_f32[:])
+            for chunk in range(PACK):
+                cols = slice(HID + chunk * P, HID + (chunk + 1) * P)
+                nc.tensor.transpose(dyn_t[:, chunk, :], rows[:, cols], ident_f32[:])
+            if i % GD_TILES == GD_TILES - 1 and (i // GD_TILES + GD_BUFS) * GD_TILES < TILES:
+                load_gd(i // GD_TILES + GD_BUFS)
+            if i % GROUP == 0 and i // GROUP + 2 < TILES // GROUP:
+                load_grad(i // GROUP + 2)
+            if i % GROUP == 0 and i // GROUP + BATCH_GROUPS < TILES // GROUP:
+                load_tau(i // GROUP + BATCH_GROUPS)
+            recip[i] = ahead.tile([P, PACK, P], F32, name="recip")
+            tg[i] = ahead.tile([P, P, PACK], F32, name="tg")
+            th[i] = ahead.tile([P, P, PACK], F32, name="th")
+            th_sq[i] = ahead.tile([P, P, PACK], F32, name="th_sq")
+            nc.scalar.activation(
+                out=recip[i][:], in_=log_s[:, :, i % BATCH, :], func=ACT.Exp, scale=-1.0
+            )
+            nc.scalar.activation(
+                out=tg[i][:], in_=gate_t[:].rearrange("p t w -> p w t"), func=ACT.Tanh, scale=0.5
+            )
+            nc.scalar.activation(
+                out=th[i][:], in_=dyn_t[:].rearrange("p t w -> p w t"), func=ACT.Tanh
+            )
+            nc.scalar.activation(out=th_sq[i][:], in_=th[i][:], func=ACT.Square)
+
+        def transpose_grad(i):
             grad_t[i] = psum.tile([P, PACK, P], BF16, name="grad_t")
             for chunk in range(PACK):
                 cols = slice(chunk * P, (chunk + 1) * P)
-                nc.tensor.transpose(gate_t[i][:, chunk, :], rows[:, cols], ident_f32[:])
-            for chunk in range(PACK):
-                cols = slice(HID + chunk * P, HID + (chunk + 1) * P)
-                nc.tensor.transpose(dyn_t[i][:, chunk, :], rows[:, cols], ident_f32[:])
-            for chunk in range(PACK):
-                cols = slice(chunk * P, (chunk + 1) * P)
                 nc.tensor.transpose(grad_t[i][:, chunk, :], grad_sb[:, i, cols], ident_bf16[:])
-            if i % GD_TILES == GD_TILES - 1 and (i // GD_TILES + GD_BUFS) * GD_TILES < TILES:
-                load_gd(i // GD_TILES + GD_BUFS)
-
-        def reciprocal(i):
-            recip[i] = work.tile([P, PACK, P], F32, name="recip")
-            nc.scalar.activation(out=recip[i][:], in_=log_s[:, :, i, :], func=ACT.Exp, scale=-1.0)
-
-        def activations(i):
-            tg[i] = work.tile([P, P, PACK], F32, name="tg")
-            th[i] = work.tile([P, P, PACK], F32, name="th")
-            th_sq[i] = work.tile([P, P, PACK], F32, name="th_sq")
-            nc.scalar.activation(
-                out=th[i][:], in_=dyn_t[i][:].rearrange("p t w -> p w t"), func=ACT.Tanh
-            )
-            nc.scalar.activation(
-                out=tg[i][:], in_=gate_t[i][:].rearrange("p t w -> p w t"), func=ACT.Tanh, scale=0.5
-            )
-            nc.scalar.activation(out=th_sq[i][:], in_=th[i][:], func=ACT.Square)
 
         def scaled_gradient(i):
             dn[i] = work.tile([P, P, PACK], F32, name="dn")
@@ -202,17 +210,21 @@ def tile_ltcattentioncell_t_v_kernel(
                 out=m[i][:], in0=tg[i][:], scalar=1.0, in1=dn[i][:], op0=ALU.add, op1=ALU.mult
             )
 
-        def gradients(i):
-            d_gd[i] = work.tile([P, HALVES, P, PACK], BF16, name="d_gd", align_bytes=64)
-            gate_part = work.tile([P, P, PACK], F32, name="gate_part")
+        def gate_factor(i):
+            gate_part[i] = work.tile([P, P, PACK], F32, name="gate_part")
             nc.vector.scalar_tensor_tensor(
-                out=gate_part[:], in0=tg[i][:], scalar=1.0, in1=m[i][:], op0=ALU.subtract, op1=ALU.mult
+                out=gate_part[i][:], in0=tg[i][:], scalar=1.0, in1=m[i][:], op0=ALU.subtract, op1=ALU.mult
             )
+
+        def dynamics_gradient(i):
+            d_gd[i] = work.tile([P, HALVES, P, PACK], BF16, name="d_gd", align_bytes=64)
             nc.vector.scalar_tensor_tensor(
                 out=d_gd[i][:, 1], in0=th_sq[i][:], scalar=1.0, in1=m[i][:], op0=ALU.subtract, op1=ALU.mult
             )
+
+        def gate_gradient(i):
             nc.vector.scalar_tensor_tensor(
-                out=d_gd[i][:, 0], in0=gate_part[:], scalar=0.5, in1=th[i][:], op0=ALU.mult, op1=ALU.mult
+                out=d_gd[i][:, 0], in0=gate_part[i][:], scalar=0.5, in1=th[i][:], op0=ALU.mult, op1=ALU.mult
             )
 
         def quantise(i):
@@ -240,24 +252,34 @@ def tile_ltcattentioncell_t_v_kernel(
                 )
 
         def write_out(i):
-            q, j = divmod(i, GROUP)
-            if j == 0:
-                out_sb[q] = store.tile([P, GROUP, IN_DIM], F32, name="out_sb")
-            nc.scalar.copy(out=out_sb[q][:, j, :], in_=acc[i][:, 0:IN_DIM])
-            if j == GROUP - 1:
-                nc.sync.dma_start(out=out_rows[:, q * GROUP : (q + 1) * GROUP, :], in_=out_sb[q][:])
+            out_sb = store.tile([P, IN_DIM], F32)
+            nc.scalar.copy(out=out_sb[:], in_=acc[i][:, 0:IN_DIM])
+            nc.sync.dma_start(out=out_rows[:, i, :], in_=out_sb[:])
 
         def run(stage, i):
             if 0 <= i < TILES:
                 stage(i)
 
-        for n in range(-2, TILES + 2):
-            run(transpose_inputs, n + 2)
-            run(activations, n + 1)
-            run(reciprocal, n + 2)
+        scalar_jobs = []
+        for batch in range(BATCHES):
+            scalar_jobs.extend((activations, i) for i in range(batch * BATCH, (batch + 1) * BATCH))
+            if batch + 1 < BATCHES:
+                groups = range((batch + 1) * BATCH_GROUPS, (batch + 2) * BATCH_GROUPS)
+                scalar_jobs.extend((logarithms, q) for q in groups)
+
+        transpose_grad(0)
+        transpose_grad(1)
+        for n in range(-LEAD, TILES + 2):
+            if n >= 0:
+                run(transpose_grad, n + 2)
+            if n + LEAD < len(scalar_jobs):
+                stage, index = scalar_jobs[n + LEAD]
+                stage(index)
             run(shared_factor, n)
             run(quantise, n - 1)
             run(multiply, n - 1)
+            run(gate_factor, n)
+            run(dynamics_gradient, n)
             run(scaled_gradient, n + 1)
-            run(gradients, n)
+            run(gate_gradient, n)
             run(write_out, n - 2)

@@ -11,19 +11,24 @@ E5M2_X4 = mybir.dt.float8_e5m2_x4
 E4M3_X4 = mybir.dt.float8_e4m3fn_x4
 ACT = mybir.ActivationFunctionType
 ALU = mybir.AluOpType
+AX = mybir.AxisListType
 
 P = 128
 TOKENS, HID, IN_DIM = 3072, 512, 256
 PACK = 4
 HALVES = 2
 TILES = TOKENS // P
+SIZES = [1] * 24
 GROUP = 4
-BATCH_GROUPS = 3
-BATCH = BATCH_GROUPS * GROUP
-BATCHES = TILES // BATCH
-LEAD = 1 + (BATCHES - 1) * BATCH_GROUPS
-GD_TILES = 2
-GD_BUFS = 4
+GROUPS = TILES // GROUP
+BATCHES = [3, 3]
+LEAD = 6
+PRE_A = 3
+SQ_VECTOR_UNITS = 0
+SQ_SCALAR_FROM = 12
+DEPTH = LEAD + 2
+GD_BUFS = 6
+STORE_BUFS = 8
 MOVING = 512
 
 FLOPS = 2 * TOKENS * HALVES * HID * IN_DIM
@@ -41,6 +46,9 @@ def tile_ltcattentioncell_t_v_kernel(
     tc, t, h_ltc, x_t, context, W_gd, b_gd, W_tau, b_tau, gleak, cm, g_d, tau, grad_out, out
 ):
     nc = tc.nc
+    units = len(SIZES)
+    firsts = [sum(SIZES[:u]) for u in range(units)]
+    unit_of = [u for u in range(units) for i in range(SIZES[u])]
     tau_rows = tau.rearrange("(p i) h -> p i h", i=TILES)
     gd_rows = g_d.rearrange("(p i) k -> p i k", i=TILES)
     grad_rows = grad_out.rearrange("(p i) h -> p i h", i=TILES)
@@ -49,12 +57,19 @@ def tile_ltcattentioncell_t_v_kernel(
     with ExitStack() as ctx:
         ctx.enter_context(tc.manual_schedule())
         const = ctx.enter_context(tc.tile_pool(name="const", bufs=1))
-        tau_pool = ctx.enter_context(tc.tile_pool(name="tau", bufs=BATCH_GROUPS))
+        tau_pool = ctx.enter_context(tc.tile_pool(name="tau", bufs=3))
         gd_pool = ctx.enter_context(tc.tile_pool(name="gd", bufs=GD_BUFS))
-        ahead = ctx.enter_context(tc.tile_pool(name="ahead", bufs=LEAD + 1))
+        ahead = ctx.enter_context(tc.tile_pool(name="ahead", bufs=DEPTH))
         work = ctx.enter_context(tc.tile_pool(name="work", bufs=3))
-        store = ctx.enter_context(tc.tile_pool(name="store", bufs=4))
-        psum = ctx.enter_context(tc.psum_pool(name="psum", bufs=2))
+        quant = ctx.enter_context(tc.tile_pool(name="quant", bufs=2))
+        store = ctx.enter_context(tc.tile_pool(name="store", bufs=STORE_BUFS))
+        psum_one = ctx.enter_context(tc.psum_pool(name="psum_one", bufs=1))
+        psum_two = ctx.enter_context(tc.psum_pool(name="psum_two", bufs=2))
+
+        zero = const.tile([P, 1], F32)
+        nc.vector.memset(zero[:], 0.0)
+        warm = const.tile([P, 1], F32)
+        nc.scalar.activation(out=warm[:], in_=zero[:], func=ACT.Sigmoid)
 
         ident_bf16 = const.tile([P, P], BF16)
         make_identity(nc, ident_bf16[:])
@@ -65,31 +80,6 @@ def tile_ltcattentioncell_t_v_kernel(
         nc.vector.memset(vec_rows[:], 0.0)
         nc.sync.dma_start(out=vec_rows[0:PACK, :], in_=cm.rearrange("(t p) -> t p", p=P))
         nc.sync.dma_start(out=vec_rows[PACK : 2 * PACK, :], in_=gleak.rearrange("(t p) -> t p", p=P))
-        vec_cols = psum.tile([P, P], BF16, tag="grad_t")
-        nc.tensor.transpose(vec_cols[:], vec_rows[:], ident_bf16[:])
-        v = const.tile([P, 2 * PACK], F32)
-        nc.vector.tensor_copy(out=v[:], in_=vec_cols[:, 0 : 2 * PACK])
-        one = const.tile([P, 1], F32)
-        nc.vector.memset(one[:], 1.0)
-        v_abs = const.tile([P, 2 * PACK], F32)
-        nc.scalar.activation(out=v_abs[:], in_=v[:], func=ACT.Abs)
-        v_exp = const.tile([P, 2 * PACK], F32)
-        nc.scalar.activation(out=v_exp[:], in_=v_abs[:], func=ACT.Exp, scale=-1.0)
-        v_log = const.tile([P, 2 * PACK], F32)
-        nc.scalar.activation(out=v_log[:], in_=v_exp[:], func=ACT.Ln, bias=one[:])
-        softplus = const.tile([P, 2 * PACK], F32)
-        nc.vector.scalar_tensor_tensor(
-            out=softplus[:], in0=v[:], scalar=0.0, in1=v_log[:], op0=ALU.max, op1=ALU.add
-        )
-        c = const.tile([P, PACK], F32)
-        nc.vector.scalar_tensor_tensor(
-            out=c[:],
-            in0=softplus[:, 0:PACK],
-            scalar=1e-6,
-            in1=softplus[:, PACK : 2 * PACK],
-            op0=ALU.add,
-            op1=ALU.add,
-        )
 
         tau_sb, gd_sb = {}, {}
         grad_sb = const.tile([P, TILES, HID], BF16)
@@ -102,47 +92,221 @@ def tile_ltcattentioncell_t_v_kernel(
             tiles = slice(q * GROUP, (q + 1) * GROUP)
             nc.sync.dma_start(out=grad_sb[:, tiles, :], in_=grad_rows[:, tiles, :])
 
-        def load_gd(k):
-            gd_sb[k] = gd_pool.tile([P, GD_TILES, HALVES * HID], F32, name="gd_sb")
-            nc.sync.dma_start(out=gd_sb[k][:], in_=gd_rows[:, k * GD_TILES : (k + 1) * GD_TILES, :])
-
-        log_s = const.tile([P, PACK, BATCH, P], F32)
-
-        def logarithms(q):
-            first = (q % BATCH_GROUPS) * GROUP
-            for chunk in range(PACK):
-                tau_t = psum.tile([P, GROUP, P], F32, tag=("gate_t", "dyn_t")[chunk % 2])
-                for j in range(GROUP):
-                    nc.tensor.transpose(
-                        tau_t[:, j, :], tau_sb[q][:, j, chunk * P : (chunk + 1) * P], ident_f32[:]
-                    )
-                nc.scalar.activation(
-                    out=log_s[:, chunk, first : first + GROUP, :],
-                    in_=tau_t[:],
-                    func=ACT.Ln,
-                    bias=c[:, chunk : chunk + 1],
-                )
+        def load_gd(u):
+            gd_sb[u] = gd_pool.tile([P, SIZES[u], HALVES * HID], F32, name="gd_sb")
+            nc.sync.dma_start(out=gd_sb[u][:], in_=gd_rows[:, firsts[u] : firsts[u] + SIZES[u], :])
 
         w_view = W_gd.rearrange("(g t p) n -> g p t n", t=PACK, p=P)
         w_raw = const.tile([P, HALVES, PACK, IN_DIM], BF16)
-        load_tau(0)
+        for u in range(PRE_A):
+            load_gd(u)
+        load_grad(0)
+        for q in range(BATCHES[0]):
+            load_tau(q)
         for half in range(HALVES):
             nc.sync.dma_start(out=w_raw[:, half], in_=w_view[half, :, :, 0:IN_DIM])
-        for q in range(1, BATCH_GROUPS):
-            load_tau(q)
-        load_grad(0)
-        for k in range(GD_BUFS):
-            load_gd(k)
+        for u in range(PRE_A, GD_BUFS):
+            load_gd(u)
         load_grad(1)
+        grads = [2]
+        taus = [BATCHES[0]]
 
-        for q in range(BATCH_GROUPS):
+        vec_cols = psum_two.tile([P, P], BF16, tag="tau_t")
+        nc.tensor.transpose(vec_cols[:], vec_rows[:], ident_bf16[:])
+        v = const.tile([P, 2 * PACK], F32)
+        nc.vector.tensor_copy(out=v[:], in_=vec_cols[:, 0 : 2 * PACK])
+        v_abs = const.tile([P, 2 * PACK], F32)
+        nc.scalar.activation(out=v_abs[:], in_=v[:], func=ACT.Abs)
+        v_sig = const.tile([P, 2 * PACK], F32)
+        nc.scalar.activation(out=v_sig[:], in_=v_abs[:], func=ACT.Sigmoid)
+        relu = const.tile([P, 2 * PACK], F32)
+        nc.vector.tensor_scalar(out=relu[:], in0=v[:], scalar1=0.0, scalar2=None, op0=ALU.max)
+        floor = const.tile([P, PACK], F32)
+        nc.vector.scalar_tensor_tensor(
+            out=floor[:], in0=relu[:, 0:PACK], scalar=1e-6, in1=relu[:, PACK : 2 * PACK], op0=ALU.add, op1=ALU.add
+        )
+        floor_min = const.tile([P, 1], F32)
+        nc.vector.tensor_reduce(out=floor_min[:], in_=floor[:], op=ALU.min, axis=AX.X)
+        floor_inv = const.tile([P, 1], F32)
+        nc.vector.reciprocal(out=floor_inv[:], in_=floor_min[:])
+        inv = const.tile([P, 1], F32)
+        nc.vector.tensor_scalar(out=inv[:], in0=floor_inv[:], scalar1=2.0, scalar2=None, op0=ALU.mult)
+        neg_inv = const.tile([P, 1], F32)
+        nc.vector.tensor_scalar(out=neg_inv[:], in0=floor_inv[:], scalar1=-2.0, scalar2=None, op0=ALU.mult)
+        bias_floor = const.tile([P, PACK], F32)
+        nc.vector.tensor_scalar(
+            out=bias_floor[:], in0=floor[:], scalar1=inv[:, 0:1], scalar2=-1.0, op0=ALU.mult, op1=ALU.add
+        )
+        sig_prod = const.tile([P, PACK], F32)
+        nc.vector.tensor_tensor(out=sig_prod[:], in0=v_sig[:, 0:PACK], in1=v_sig[:, PACK : 2 * PACK], op=ALU.mult)
+
+        log_rs = const.tile([P, PACK, TILES, P], F32)
+        sgth, kq = {}, {}
+        banks = {}
+        m, x2, d_gd, codes, scales, acc, out_sb = {}, {}, {}, {}, {}, {}, {}
+
+        def logarithm(q, chunk):
+            tau_t = psum_two.tile([P, GROUP, P], F32, tag="tau_t")
+            for j in range(GROUP):
+                nc.tensor.transpose(tau_t[:, j, :], tau_sb[q][:, j, chunk * P : (chunk + 1) * P], ident_f32[:])
+            nc.scalar.activation(
+                out=log_rs[:, chunk, q * GROUP : (q + 1) * GROUP, :],
+                in_=tau_t[:],
+                func=ACT.Ln,
+                scale=inv[:, 0:1],
+                bias=ln_bias[:, chunk : chunk + 1],
+            )
+
+        def reciprocals(u):
+            if not 0 <= u < units:
+                return
+            view = log_rs[:, :, firsts[u] : firsts[u] + SIZES[u], :]
+            nc.scalar.activation(out=view, in_=view, func=ACT.Sigmoid, scale=-1.0)
+
+        def activations(u):
+            if not 0 <= u < units:
+                return
+            sgth[u] = ahead.tile([P, SIZES[u], HALVES * HID], F32, name="sgth")
+            kq[u] = ahead.tile([P, SIZES[u], HALVES * HID], F32, name="kq")
+            nc.scalar.activation(out=sgth[u][:, :, HID:], in_=gd_sb[u][:, :, HID:], func=ACT.Tanh)
+            if u < SQ_VECTOR_UNITS:
+                nc.vector.tensor_tensor(
+                    out=kq[u][:, :, HID:], in0=sgth[u][:, :, HID:], in1=sgth[u][:, :, HID:], op=ALU.mult
+                )
+            elif u >= SQ_SCALAR_FROM:
+                nc.scalar.activation(out=kq[u][:, :, HID:], in_=sgth[u][:, :, HID:], func=ACT.Square)
+            else:
+                nc.gpsimd.tensor_tensor(
+                    out=kq[u][:, :, HID:], in0=sgth[u][:, :, HID:], in1=sgth[u][:, :, HID:], op=ALU.mult
+                )
+            nc.scalar.activation(out=sgth[u][:, :, 0:HID], in_=gd_sb[u][:, :, 0:HID], func=ACT.Sigmoid)
+            nc.gpsimd.tensor_tensor(
+                out=kq[u][:, :, 0:HID],
+                in0=grad_sb[:, firsts[u] : firsts[u] + SIZES[u], :],
+                in1=sgth[u][:, :, 0:HID],
+                op=ALU.mult,
+            )
+            nxt = u + GD_BUFS
+            if nxt < units:
+                last_tile = firsts[nxt] + SIZES[nxt] - 1
+                while grads[0] < GROUPS and grads[0] * GROUP <= last_tile:
+                    load_grad(grads[0])
+                    grads[0] += 1
+                load_gd(nxt)
+
+        def flip(what, i):
+            if not 0 <= i < TILES:
+                return
+            src = {"k": kq, "thsq": kq, "sg": sgth, "th": sgth}[what][unit_of[i]]
+            first = {"k": 0, "sg": 0, "thsq": HID, "th": HID}[what]
+            bank = psum_one.tile([P, PACK, P], F32, tag=what)
+            for chunk in range(PACK):
+                cols = slice(first + chunk * P, first + (chunk + 1) * P)
+                nc.tensor.transpose(bank[:, chunk, :], src[:, i - firsts[unit_of[i]], cols], ident_f32[:])
+            banks[what, i] = bank
+
+        def by_token(bank):
+            return bank[:].rearrange("p t w -> p w t")
+
+        def shared(i):
+            if not 0 <= i < TILES:
+                return
+            m[i] = work.tile([P, P, PACK], F32, name="m")
+            nc.vector.scalar_tensor_tensor(
+                out=m[i][:],
+                in0=by_token(banks["k", i]),
+                scalar=neg_inv[:, 0:1],
+                in1=log_rs[:, :, i, :].rearrange("p t w -> p w t"),
+                op0=ALU.mult,
+                op1=ALU.mult,
+            )
+
+        def gate_factor(i):
+            x2[i] = work.tile([P, P, PACK], F32, name="x2")
+            nc.vector.scalar_tensor_tensor(
+                out=x2[i][:], in0=by_token(banks["sg", i]), scalar=1.0, in1=m[i][:], op0=ALU.subtract, op1=ALU.mult
+            )
+
+        def dynamics_gradient(i):
+            u = unit_of[i]
+            if i == firsts[u]:
+                d_gd[u] = quant.tile([P, SIZES[u], HALVES, P, PACK], BF16, name="d_gd", align_bytes=64)
+            nc.vector.scalar_tensor_tensor(
+                out=d_gd[u][:, i - firsts[u], 1],
+                in0=by_token(banks["thsq", i]),
+                scalar=1.0,
+                in1=m[i][:],
+                op0=ALU.subtract,
+                op1=ALU.mult,
+            )
+
+        def gate_gradient(i):
+            u = unit_of[i]
+            nc.vector.tensor_tensor(
+                out=d_gd[u][:, i - firsts[u], 0], in0=by_token(banks["th", i]), in1=x2[i][:], op=ALU.mult
+            )
+
+        def quantise(u):
+            codes[u] = quant.tile([P, SIZES[u] * HALVES * P], U32, name="codes", align_bytes=64)
+            scales[u] = quant.tile([P, SIZES[u] * HALVES * P], U8, name="scales", align_bytes=64)
+            nc.vector.quantize_mx(
+                out=codes[u][:].bitcast(E5M2_X4),
+                scales=scales[u][:],
+                in_=d_gd[u][:].rearrange("p j g w t -> p (j g w t)"),
+            )
+
+        def multiply(u):
+            for j in range(SIZES[u]):
+                acc[u, j] = psum_two.tile([P, MOVING], F32, name="acc")
+                for half in range(HALVES):
+                    tokens = slice((j * HALVES + half) * P, (j * HALVES + half + 1) * P)
+                    w_cols = slice(half * IN_DIM, half * IN_DIM + MOVING)
+                    nc.tensor.matmul_mx(
+                        out=acc[u, j][:],
+                        lhsT=codes[u][:, tokens].bitcast(E5M2_X4),
+                        lhsT_scale=scales[u][:, tokens],
+                        rhs=w_codes[:, w_cols].bitcast(E4M3_X4),
+                        rhs_scale=w_scales[:, w_cols],
+                        start=(half == 0),
+                        stop=(half == HALVES - 1),
+                    )
+
+        def write_out(u, on_vector):
+            if not 0 <= u < units:
+                return
+            out_sb[u] = store.tile([P, SIZES[u], IN_DIM], F32, name="out_sb")
+            for j in range(SIZES[u]):
+                if on_vector:
+                    nc.vector.tensor_copy(out=out_sb[u][:, j, :], in_=acc[u, j][:, 0:IN_DIM])
+                else:
+                    nc.scalar.copy(out=out_sb[u][:, j, :], in_=acc[u, j][:, 0:IN_DIM])
+            nc.sync.dma_start(out=out_rows[:, firsts[u] : firsts[u] + SIZES[u], :], in_=out_sb[u][:])
+
+        for u in range(PRE_A):
+            activations(u)
+        sig_log = const.tile([P, PACK], F32)
+        nc.scalar.activation(out=sig_log[:], in_=sig_prod[:], func=ACT.Ln)
+        ln_bias = const.tile([P, PACK], F32)
+        for chunk in range(PACK):
+            nc.vector.tensor_scalar(
+                out=ln_bias[:, chunk : chunk + 1],
+                in0=sig_log[:, chunk : chunk + 1],
+                scalar1=neg_inv[:, 0:1],
+                scalar2=bias_floor[:, chunk : chunk + 1],
+                op0=ALU.mult,
+                op1=ALU.add,
+            )
+
+        def logarithms(q):
+            for chunk in range(PACK):
+                logarithm(q, chunk)
+
+        for q in range(BATCHES[0]):
             logarithms(q)
 
         w_grouped = const.tile([P, HALVES, IN_DIM, PACK], BF16, align_bytes=64)
         for half in range(HALVES):
-            nc.vector.tensor_copy(
-                out=w_grouped[:, half], in_=w_raw[:, half].rearrange("p t n -> p n t")
-            )
+            nc.vector.tensor_copy(out=w_grouped[:, half], in_=w_raw[:, half].rearrange("p t n -> p n t"))
         w_codes = const.tile([P, 2 * HALVES * IN_DIM], U32, align_bytes=64)
         w_scales = const.tile([P, 2 * HALVES * IN_DIM], U8, align_bytes=64)
         for copy in range(2):
@@ -153,133 +317,58 @@ def tile_ltcattentioncell_t_v_kernel(
                 in_=w_grouped[:].rearrange("p g n t -> p (g n t)"),
             )
 
-        grad_t, acc = {}, {}
-        recip, tg, th, th_sq, dn, m, gate_part, d_gd, codes, scales = {}, {}, {}, {}, {}, {}, {}, {}, {}, {}
+        def tile_job(i):
+            reciprocals(i)
+            if i >= PRE_A:
+                activations(i)
 
-        def activations(i):
-            rows = gd_sb[i // GD_TILES][:, i % GD_TILES, :]
-            gate_t = psum.tile([P, PACK, P], F32)
-            dyn_t = psum.tile([P, PACK, P], F32)
-            for chunk in range(PACK):
-                cols = slice(chunk * P, (chunk + 1) * P)
-                nc.tensor.transpose(gate_t[:, chunk, :], rows[:, cols], ident_f32[:])
-            for chunk in range(PACK):
-                cols = slice(HID + chunk * P, HID + (chunk + 1) * P)
-                nc.tensor.transpose(dyn_t[:, chunk, :], rows[:, cols], ident_f32[:])
-            if i % GD_TILES == GD_TILES - 1 and (i // GD_TILES + GD_BUFS) * GD_TILES < TILES:
-                load_gd(i // GD_TILES + GD_BUFS)
-            if i % GROUP == 0 and i // GROUP + 2 < TILES // GROUP:
-                load_grad(i // GROUP + 2)
-            if i % GROUP == 0 and i // GROUP + BATCH_GROUPS < TILES // GROUP:
-                load_tau(i // GROUP + BATCH_GROUPS)
-            recip[i] = ahead.tile([P, PACK, P], F32, name="recip")
-            tg[i] = ahead.tile([P, P, PACK], F32, name="tg")
-            th[i] = ahead.tile([P, P, PACK], F32, name="th")
-            th_sq[i] = ahead.tile([P, P, PACK], F32, name="th_sq")
-            nc.scalar.activation(
-                out=recip[i][:], in_=log_s[:, :, i % BATCH, :], func=ACT.Exp, scale=-1.0
-            )
-            nc.scalar.activation(
-                out=tg[i][:], in_=gate_t[:].rearrange("p t w -> p w t"), func=ACT.Tanh, scale=0.5
-            )
-            nc.scalar.activation(
-                out=th[i][:], in_=dyn_t[:].rearrange("p t w -> p w t"), func=ACT.Tanh
-            )
-            nc.scalar.activation(out=th_sq[i][:], in_=th[i][:], func=ACT.Square)
+        jobs = []
+        done = 0
+        for b in range(len(BATCHES)):
+            jobs.extend((tile_job, i) for i in range(done * GROUP, (done + BATCHES[b]) * GROUP))
+            done += BATCHES[b]
+            if b + 1 < len(BATCHES):
+                jobs.extend((logarithms, q) for q in range(done, done + BATCHES[b + 1]))
 
-        def transpose_grad(i):
-            grad_t[i] = psum.tile([P, PACK, P], BF16, name="grad_t")
-            for chunk in range(PACK):
-                cols = slice(chunk * P, (chunk + 1) * P)
-                nc.tensor.transpose(grad_t[i][:, chunk, :], grad_sb[:, i, cols], ident_bf16[:])
-
-        def scaled_gradient(i):
-            dn[i] = work.tile([P, P, PACK], F32, name="dn")
-            nc.vector.scalar_tensor_tensor(
-                out=dn[i][:],
-                in0=grad_t[i][:].rearrange("p t w -> p w t"),
-                scalar=-0.5,
-                in1=recip[i][:].rearrange("p t w -> p w t"),
-                op0=ALU.mult,
-                op1=ALU.mult,
-            )
-
-        def shared_factor(i):
-            m[i] = work.tile([P, P, PACK], F32, name="m")
-            nc.vector.scalar_tensor_tensor(
-                out=m[i][:], in0=tg[i][:], scalar=1.0, in1=dn[i][:], op0=ALU.add, op1=ALU.mult
-            )
-
-        def gate_factor(i):
-            gate_part[i] = work.tile([P, P, PACK], F32, name="gate_part")
-            nc.vector.scalar_tensor_tensor(
-                out=gate_part[i][:], in0=tg[i][:], scalar=1.0, in1=m[i][:], op0=ALU.subtract, op1=ALU.mult
-            )
-
-        def dynamics_gradient(i):
-            d_gd[i] = work.tile([P, HALVES, P, PACK], BF16, name="d_gd", align_bytes=64)
-            nc.vector.scalar_tensor_tensor(
-                out=d_gd[i][:, 1], in0=th_sq[i][:], scalar=1.0, in1=m[i][:], op0=ALU.subtract, op1=ALU.mult
-            )
-
-        def gate_gradient(i):
-            nc.vector.scalar_tensor_tensor(
-                out=d_gd[i][:, 0], in0=gate_part[i][:], scalar=0.5, in1=th[i][:], op0=ALU.mult, op1=ALU.mult
-            )
-
-        def quantise(i):
-            codes[i] = work.tile([P, HALVES * P], U32, name="codes", align_bytes=64)
-            scales[i] = work.tile([P, HALVES * P], U8, name="scales", align_bytes=64)
-            nc.vector.quantize_mx(
-                out=codes[i][:].bitcast(E5M2_X4),
-                scales=scales[i][:],
-                in_=d_gd[i][:].rearrange("p g w t -> p (g w t)"),
-            )
-
-        def multiply(i):
-            acc[i] = psum.tile([P, MOVING], F32, name="acc")
-            for half in range(HALVES):
-                tokens = slice(half * P, (half + 1) * P)
-                w_cols = slice(half * IN_DIM, half * IN_DIM + MOVING)
-                nc.tensor.matmul_mx(
-                    out=acc[i][:],
-                    lhsT=codes[i][:, tokens].bitcast(E5M2_X4),
-                    lhsT_scale=scales[i][:, tokens],
-                    rhs=w_codes[:, w_cols].bitcast(E4M3_X4),
-                    rhs_scale=w_scales[:, w_cols],
-                    start=(half == 0),
-                    stop=(half == HALVES - 1),
-                )
-
-        def write_out(i):
-            out_sb = store.tile([P, IN_DIM], F32)
-            nc.scalar.copy(out=out_sb[:], in_=acc[i][:, 0:IN_DIM])
-            nc.sync.dma_start(out=out_rows[:, i, :], in_=out_sb[:])
-
-        def run(stage, i):
-            if 0 <= i < TILES:
-                stage(i)
-
-        scalar_jobs = []
-        for batch in range(BATCHES):
-            scalar_jobs.extend((activations, i) for i in range(batch * BATCH, (batch + 1) * BATCH))
-            if batch + 1 < BATCHES:
-                groups = range((batch + 1) * BATCH_GROUPS, (batch + 2) * BATCH_GROUPS)
-                scalar_jobs.extend((logarithms, q) for q in groups)
-
-        transpose_grad(0)
-        transpose_grad(1)
-        for n in range(-LEAD, TILES + 2):
-            if n >= 0:
-                run(transpose_grad, n + 2)
-            if n + LEAD < len(scalar_jobs):
-                stage, index = scalar_jobs[n + LEAD]
-                stage(index)
-            run(shared_factor, n)
-            run(quantise, n - 1)
-            run(multiply, n - 1)
-            run(gate_factor, n)
-            run(dynamics_gradient, n)
-            run(scaled_gradient, n + 1)
-            run(gate_gradient, n)
-            run(write_out, n - 2)
+        for n in range(-LEAD, TILES):
+            group = None
+            if n + LEAD < len(jobs):
+                stage, index = jobs[n + LEAD]
+                if stage == tile_job and index % GROUP == 0 and taus[0] < GROUPS:
+                    load_tau(taus[0])
+                    taus[0] += 1
+                if stage == logarithms and n >= 0:
+                    group = index
+                else:
+                    stage(index)
+            if n == -1:
+                for what in ("thsq", "k", "sg", "th"):
+                    flip(what, 0)
+                shared(0)
+                flip("k", 1)
+            if n < 0:
+                continue
+            write_out(n - 2, False)
+            gate_factor(n)
+            flip("sg", n + 1)
+            if group is not None:
+                logarithm(group, 0)
+            if n >= 1:
+                quantise(n - 1)
+                multiply(n - 1)
+            dynamics_gradient(n)
+            flip("thsq", n + 1)
+            if group is not None:
+                logarithm(group, 1)
+            shared(n + 1)
+            flip("k", n + 2)
+            if group is not None:
+                logarithm(group, 2)
+            gate_gradient(n)
+            flip("th", n + 1)
+            if group is not None:
+                logarithm(group, 3)
+        quantise(TILES - 1)
+        multiply(TILES - 1)
+        write_out(TILES - 2, False)
+        write_out(TILES - 1, False)

@@ -24,6 +24,7 @@ GROUPS = TILES // GROUP
 BATCHES = [3, 3]
 LEAD = 6
 PRE_A = 3
+EARLY = 1
 SQ_VECTOR_UNITS = 0
 SQ_SCALAR_FROM = 12
 DEPTH = LEAD + 2
@@ -145,8 +146,8 @@ def tile_ltcattentioncell_t_v_kernel(
         banks = {}
         m, x2, d_gd, codes, scales, acc, out_sb = {}, {}, {}, {}, {}, {}, {}
 
-        def logarithm(q, chunk):
-            tau_t = psum_two.tile([P, GROUP, P], F32, tag="tau_t")
+        def logarithm(q, chunk, tag="tau_t"):
+            tau_t = psum_two.tile([P, GROUP, P], F32, tag=tag)
             for j in range(GROUP):
                 nc.tensor.transpose(tau_t[:, j, :], tau_sb[q][:, j, chunk * P : (chunk + 1) * P], ident_f32[:])
             nc.scalar.activation(
@@ -302,7 +303,8 @@ def tile_ltcattentioncell_t_v_kernel(
                 logarithm(q, chunk)
 
         for q in range(BATCHES[0]):
-            logarithms(q)
+            for chunk in range(PACK):
+                logarithm(q, chunk, ("tau_t", "acc")[chunk % 2])
 
         w_grouped = const.tile([P, HALVES, IN_DIM, PACK], BF16, align_bytes=64)
         for half in range(HALVES):
@@ -317,10 +319,14 @@ def tile_ltcattentioncell_t_v_kernel(
                 in_=w_grouped[:].rearrange("p g n t -> p (g n t)"),
             )
 
+        first_batch = BATCHES[0] * GROUP
+
         def tile_job(i):
             reciprocals(i)
-            if i >= PRE_A:
+            if PRE_A <= i < first_batch:
                 activations(i)
+            if i + EARLY >= first_batch:
+                activations(i + EARLY)
 
         jobs = []
         done = 0
@@ -332,6 +338,7 @@ def tile_ltcattentioncell_t_v_kernel(
 
         for n in range(-LEAD, TILES):
             group = None
+            write_out(n - 2, False)
             if n + LEAD < len(jobs):
                 stage, index = jobs[n + LEAD]
                 if stage == tile_job and index % GROUP == 0 and taus[0] < GROUPS:
@@ -348,7 +355,6 @@ def tile_ltcattentioncell_t_v_kernel(
                 flip("k", 1)
             if n < 0:
                 continue
-            write_out(n - 2, False)
             gate_factor(n)
             flip("sg", n + 1)
             if group is not None:

@@ -27,9 +27,13 @@ PRE_A = 3
 EARLY = 1
 SQ_VECTOR_UNITS = 0
 SQ_SCALAR_FROM = 12
+SQ_SCALAR_EVERY = 99
 DEPTH = LEAD + 2
-GD_BUFS = 6
-STORE_BUFS = 8
+GD_BUFS = 5
+STORE_BUFS = 6
+CODE_BUFS = 7
+CATCH_UP = 2
+RESUME = 2
 MOVING = 512
 
 FLOPS = 2 * TOKENS * HALVES * HID * IN_DIM
@@ -63,6 +67,7 @@ def tile_ltcattentioncell_t_v_kernel(
         ahead = ctx.enter_context(tc.tile_pool(name="ahead", bufs=DEPTH))
         work = ctx.enter_context(tc.tile_pool(name="work", bufs=3))
         quant = ctx.enter_context(tc.tile_pool(name="quant", bufs=2))
+        coded = ctx.enter_context(tc.tile_pool(name="coded", bufs=CODE_BUFS))
         store = ctx.enter_context(tc.tile_pool(name="store", bufs=STORE_BUFS))
         psum_one = ctx.enter_context(tc.psum_pool(name="psum_one", bufs=1))
         psum_two = ctx.enter_context(tc.psum_pool(name="psum_two", bufs=2))
@@ -101,8 +106,9 @@ def tile_ltcattentioncell_t_v_kernel(
         w_raw = const.tile([P, HALVES, PACK, IN_DIM], BF16)
         for u in range(PRE_A):
             load_gd(u)
+        load_tau(0)
         load_grad(0)
-        for q in range(BATCHES[0]):
+        for q in range(1, BATCHES[0]):
             load_tau(q)
         for half in range(HALVES):
             nc.sync.dma_start(out=w_raw[:, half], in_=w_view[half, :, :, 0:IN_DIM])
@@ -174,7 +180,7 @@ def tile_ltcattentioncell_t_v_kernel(
                 nc.vector.tensor_tensor(
                     out=kq[u][:, :, HID:], in0=sgth[u][:, :, HID:], in1=sgth[u][:, :, HID:], op=ALU.mult
                 )
-            elif u >= SQ_SCALAR_FROM:
+            elif u >= SQ_SCALAR_FROM and (u - SQ_SCALAR_FROM) % SQ_SCALAR_EVERY != SQ_SCALAR_EVERY - 1:
                 nc.scalar.activation(out=kq[u][:, :, HID:], in_=sgth[u][:, :, HID:], func=ACT.Square)
             else:
                 nc.gpsimd.tensor_tensor(
@@ -248,8 +254,8 @@ def tile_ltcattentioncell_t_v_kernel(
             )
 
         def quantise(u):
-            codes[u] = quant.tile([P, SIZES[u] * HALVES * P], U32, name="codes", align_bytes=64)
-            scales[u] = quant.tile([P, SIZES[u] * HALVES * P], U8, name="scales", align_bytes=64)
+            codes[u] = coded.tile([P, SIZES[u] * HALVES * P], U32, name="codes", align_bytes=64)
+            scales[u] = coded.tile([P, SIZES[u] * HALVES * P], U8, name="scales", align_bytes=64)
             nc.vector.quantize_mx(
                 out=codes[u][:].bitcast(E5M2_X4),
                 scales=scales[u][:],
@@ -336,9 +342,22 @@ def tile_ltcattentioncell_t_v_kernel(
             if b + 1 < len(BATCHES):
                 jobs.extend((logarithms, q) for q in range(done, done + BATCHES[b + 1]))
 
+        multiplied, copied, hold = [0], [0], [-1]
+
+        def copy_products():
+            while copied[0] < multiplied[0]:
+                write_out(copied[0], False)
+                copied[0] += 1
+
+        def multiply_products(ready, most):
+            for count in range(most):
+                if multiplied[0] < ready:
+                    multiply(multiplied[0])
+                    multiplied[0] += 1
+
         for n in range(-LEAD, TILES):
             group = None
-            write_out(n - 2, False)
+            copy_products()
             if n + LEAD < len(jobs):
                 stage, index = jobs[n + LEAD]
                 if stage == tile_job and index % GROUP == 0 and taus[0] < GROUPS:
@@ -358,23 +377,27 @@ def tile_ltcattentioncell_t_v_kernel(
             gate_factor(n)
             flip("sg", n + 1)
             if group is not None:
-                logarithm(group, 0)
+                logarithm(group, 0, "tau_t")
             if n >= 1:
                 quantise(n - 1)
-                multiply(n - 1)
+                if group is not None:
+                    hold[0] = n + RESUME
+                if n > hold[0]:
+                    multiply_products(n, CATCH_UP)
             dynamics_gradient(n)
             flip("thsq", n + 1)
             if group is not None:
-                logarithm(group, 1)
+                logarithm(group, 1, "acc")
             shared(n + 1)
             flip("k", n + 2)
             if group is not None:
-                logarithm(group, 2)
+                logarithm(group, 2, "tau_t")
             gate_gradient(n)
             flip("th", n + 1)
             if group is not None:
-                logarithm(group, 3)
+                logarithm(group, 3, "acc")
+        copy_products()
         quantise(TILES - 1)
-        multiply(TILES - 1)
-        write_out(TILES - 2, False)
-        write_out(TILES - 1, False)
+        multiply_products(TILES, CATCH_UP)
+        copy_products()
+        assert multiplied[0] == TILES

from contextlib import ExitStack

import concourse.mybir as mybir
from concourse.masks import make_identity

F32 = mybir.dt.float32
BF16 = mybir.dt.bfloat16
U32 = mybir.dt.uint32
U8 = mybir.dt.uint8
E5M2_X4 = mybir.dt.float8_e5m2_x4
E4M3_X4 = mybir.dt.float8_e4m3fn_x4
ACT = mybir.ActivationFunctionType
ALU = mybir.AluOpType
AX = mybir.AxisListType

P = 128
TOKENS, HID, IN_DIM = 3072, 512, 256
PACK = 4
HALVES = 2
TILES = TOKENS // P
SIZES = [1] * 24
GROUP = 4
GROUPS = TILES // GROUP
BATCHES = [3, 3]
LEAD = 6
PRE_A = 3
EARLY = 1
SQ_VECTOR_UNITS = 0
SQ_SCALAR_FROM = 12
SQ_SCALAR_EVERY = 99
DEPTH = LEAD + 2
GD_BUFS = 5
STORE_BUFS = 6
CODE_BUFS = 7
CATCH_UP = 2
RESUME = 2
MOVING = 512

FLOPS = 2 * TOKENS * HALVES * HID * IN_DIM
BYTES = (
    TOKENS * HALVES * HID * 4
    + TOKENS * HID * 4
    + TOKENS * HID * 2
    + HALVES * HID * IN_DIM * 2
    + 2 * HID * 2
    + TOKENS * IN_DIM * 4
)


def tile_ltcattentioncell_t_v_kernel(
    tc, t, h_ltc, x_t, context, W_gd, b_gd, W_tau, b_tau, gleak, cm, g_d, tau, grad_out, out
):
    nc = tc.nc
    units = len(SIZES)
    firsts = [sum(SIZES[:u]) for u in range(units)]
    unit_of = [u for u in range(units) for i in range(SIZES[u])]
    tau_rows = tau.rearrange("(p i) h -> p i h", i=TILES)
    gd_rows = g_d.rearrange("(p i) k -> p i k", i=TILES)
    grad_rows = grad_out.rearrange("(p i) h -> p i h", i=TILES)
    out_rows = out.rearrange("(p i) n -> p i n", i=TILES)

    with ExitStack() as ctx:
        ctx.enter_context(tc.manual_schedule())
        const = ctx.enter_context(tc.tile_pool(name="const", bufs=1))
        tau_pool = ctx.enter_context(tc.tile_pool(name="tau", bufs=3))
        gd_pool = ctx.enter_context(tc.tile_pool(name="gd", bufs=GD_BUFS))
        ahead = ctx.enter_context(tc.tile_pool(name="ahead", bufs=DEPTH))
        work = ctx.enter_context(tc.tile_pool(name="work", bufs=3))
        quant = ctx.enter_context(tc.tile_pool(name="quant", bufs=2))
        coded = ctx.enter_context(tc.tile_pool(name="coded", bufs=CODE_BUFS))
        store = ctx.enter_context(tc.tile_pool(name="store", bufs=STORE_BUFS))
        psum_one = ctx.enter_context(tc.psum_pool(name="psum_one", bufs=1))
        psum_two = ctx.enter_context(tc.psum_pool(name="psum_two", bufs=2))

        zero = const.tile([P, 1], F32)
        nc.vector.memset(zero[:], 0.0)
        warm = const.tile([P, 1], F32)
        nc.scalar.activation(out=warm[:], in_=zero[:], func=ACT.Sigmoid)

        ident_bf16 = const.tile([P, P], BF16)
        make_identity(nc, ident_bf16[:])
        ident_f32 = const.tile([P, P], F32)
        make_identity(nc, ident_f32[:])

        vec_rows = const.tile([P, P], BF16)
        nc.vector.memset(vec_rows[:], 0.0)
        nc.sync.dma_start(out=vec_rows[0:PACK, :], in_=cm.rearrange("(t p) -> t p", p=P))
        nc.sync.dma_start(out=vec_rows[PACK : 2 * PACK, :], in_=gleak.rearrange("(t p) -> t p", p=P))

        tau_sb, gd_sb = {}, {}
        grad_sb = const.tile([P, TILES, HID], BF16)

        def load_tau(q):
            tau_sb[q] = tau_pool.tile([P, GROUP, HID], F32, name="tau_sb")
            nc.sync.dma_start(out=tau_sb[q][:], in_=tau_rows[:, q * GROUP : (q + 1) * GROUP, :])

        def load_grad(q):
            tiles = slice(q * GROUP, (q + 1) * GROUP)
            nc.sync.dma_start(out=grad_sb[:, tiles, :], in_=grad_rows[:, tiles, :])

        def load_gd(u):
            gd_sb[u] = gd_pool.tile([P, SIZES[u], HALVES * HID], F32, name="gd_sb")
            nc.sync.dma_start(out=gd_sb[u][:], in_=gd_rows[:, firsts[u] : firsts[u] + SIZES[u], :])

        w_view = W_gd.rearrange("(g t p) n -> g p t n", t=PACK, p=P)
        w_raw = const.tile([P, HALVES, PACK, IN_DIM], BF16)
        for u in range(PRE_A):
            load_gd(u)
        load_tau(0)
        load_grad(0)
        for q in range(1, BATCHES[0]):
            load_tau(q)
        for half in range(HALVES):
            nc.sync.dma_start(out=w_raw[:, half], in_=w_view[half, :, :, 0:IN_DIM])
        for u in range(PRE_A, GD_BUFS):
            load_gd(u)
        load_grad(1)
        grads = [2]
        taus = [BATCHES[0]]

        vec_cols = psum_two.tile([P, P], BF16, tag="tau_t")
        nc.tensor.transpose(vec_cols[:], vec_rows[:], ident_bf16[:])
        v = const.tile([P, 2 * PACK], F32)
        nc.vector.tensor_copy(out=v[:], in_=vec_cols[:, 0 : 2 * PACK])
        v_abs = const.tile([P, 2 * PACK], F32)
        nc.scalar.activation(out=v_abs[:], in_=v[:], func=ACT.Abs)
        v_sig = const.tile([P, 2 * PACK], F32)
        nc.scalar.activation(out=v_sig[:], in_=v_abs[:], func=ACT.Sigmoid)
        relu = const.tile([P, 2 * PACK], F32)
        nc.vector.tensor_scalar(out=relu[:], in0=v[:], scalar1=0.0, scalar2=None, op0=ALU.max)
        floor = const.tile([P, PACK], F32)
        nc.vector.scalar_tensor_tensor(
            out=floor[:], in0=relu[:, 0:PACK], scalar=1e-6, in1=relu[:, PACK : 2 * PACK], op0=ALU.add, op1=ALU.add
        )
        floor_min = const.tile([P, 1], F32)
        nc.vector.tensor_reduce(out=floor_min[:], in_=floor[:], op=ALU.min, axis=AX.X)
        floor_inv = const.tile([P, 1], F32)
        nc.vector.reciprocal(out=floor_inv[:], in_=floor_min[:])
        inv = const.tile([P, 1], F32)
        nc.vector.tensor_scalar(out=inv[:], in0=floor_inv[:], scalar1=2.0, scalar2=None, op0=ALU.mult)
        neg_inv = const.tile([P, 1], F32)
        nc.vector.tensor_scalar(out=neg_inv[:], in0=floor_inv[:], scalar1=-2.0, scalar2=None, op0=ALU.mult)
        bias_floor = const.tile([P, PACK], F32)
        nc.vector.tensor_scalar(
            out=bias_floor[:], in0=floor[:], scalar1=inv[:, 0:1], scalar2=-1.0, op0=ALU.mult, op1=ALU.add
        )
        sig_prod = const.tile([P, PACK], F32)
        nc.vector.tensor_tensor(out=sig_prod[:], in0=v_sig[:, 0:PACK], in1=v_sig[:, PACK : 2 * PACK], op=ALU.mult)

        log_rs = const.tile([P, PACK, TILES, P], F32)
        sgth, kq = {}, {}
        banks = {}
        m, x2, d_gd, codes, scales, acc, out_sb = {}, {}, {}, {}, {}, {}, {}

        def logarithm(q, chunk, tag="tau_t"):
            tau_t = psum_two.tile([P, GROUP, P], F32, tag=tag)
            for j in range(GROUP):
                nc.tensor.transpose(tau_t[:, j, :], tau_sb[q][:, j, chunk * P : (chunk + 1) * P], ident_f32[:])
            nc.scalar.activation(
                out=log_rs[:, chunk, q * GROUP : (q + 1) * GROUP, :],
                in_=tau_t[:],
                func=ACT.Ln,
                scale=inv[:, 0:1],
                bias=ln_bias[:, chunk : chunk + 1],
            )

        def reciprocals(u):
            if not 0 <= u < units:
                return
            view = log_rs[:, :, firsts[u] : firsts[u] + SIZES[u], :]
            nc.scalar.activation(out=view, in_=view, func=ACT.Sigmoid, scale=-1.0)

        def activations(u):
            if not 0 <= u < units:
                return
            sgth[u] = ahead.tile([P, SIZES[u], HALVES * HID], F32, name="sgth")
            kq[u] = ahead.tile([P, SIZES[u], HALVES * HID], F32, name="kq")
            nc.scalar.activation(out=sgth[u][:, :, HID:], in_=gd_sb[u][:, :, HID:], func=ACT.Tanh)
            if u < SQ_VECTOR_UNITS:
                nc.vector.tensor_tensor(
                    out=kq[u][:, :, HID:], in0=sgth[u][:, :, HID:], in1=sgth[u][:, :, HID:], op=ALU.mult
                )
            elif u >= SQ_SCALAR_FROM and (u - SQ_SCALAR_FROM) % SQ_SCALAR_EVERY != SQ_SCALAR_EVERY - 1:
                nc.scalar.activation(out=kq[u][:, :, HID:], in_=sgth[u][:, :, HID:], func=ACT.Square)
            else:
                nc.gpsimd.tensor_tensor(
                    out=kq[u][:, :, HID:], in0=sgth[u][:, :, HID:], in1=sgth[u][:, :, HID:], op=ALU.mult
                )
            nc.scalar.activation(out=sgth[u][:, :, 0:HID], in_=gd_sb[u][:, :, 0:HID], func=ACT.Sigmoid)
            nc.gpsimd.tensor_tensor(
                out=kq[u][:, :, 0:HID],
                in0=grad_sb[:, firsts[u] : firsts[u] + SIZES[u], :],
                in1=sgth[u][:, :, 0:HID],
                op=ALU.mult,
            )
            nxt = u + GD_BUFS
            if nxt < units:
                last_tile = firsts[nxt] + SIZES[nxt] - 1
                while grads[0] < GROUPS and grads[0] * GROUP <= last_tile:
                    load_grad(grads[0])
                    grads[0] += 1
                load_gd(nxt)

        def flip(what, i):
            if not 0 <= i < TILES:
                return
            src = {"k": kq, "thsq": kq, "sg": sgth, "th": sgth}[what][unit_of[i]]
            first = {"k": 0, "sg": 0, "thsq": HID, "th": HID}[what]
            bank = psum_one.tile([P, PACK, P], F32, tag=what)
            for chunk in range(PACK):
                cols = slice(first + chunk * P, first + (chunk + 1) * P)
                nc.tensor.transpose(bank[:, chunk, :], src[:, i - firsts[unit_of[i]], cols], ident_f32[:])
            banks[what, i] = bank

        def by_token(bank):
            return bank[:].rearrange("p t w -> p w t")

        def shared(i):
            if not 0 <= i < TILES:
                return
            m[i] = work.tile([P, P, PACK], F32, name="m")
            nc.vector.scalar_tensor_tensor(
                out=m[i][:],
                in0=by_token(banks["k", i]),
                scalar=neg_inv[:, 0:1],
                in1=log_rs[:, :, i, :].rearrange("p t w -> p w t"),
                op0=ALU.mult,
                op1=ALU.mult,
            )

        def gate_factor(i):
            x2[i] = work.tile([P, P, PACK], F32, name="x2")
            nc.vector.scalar_tensor_tensor(
                out=x2[i][:], in0=by_token(banks["sg", i]), scalar=1.0, in1=m[i][:], op0=ALU.subtract, op1=ALU.mult
            )

        def dynamics_gradient(i):
            u = unit_of[i]
            if i == firsts[u]:
                d_gd[u] = quant.tile([P, SIZES[u], HALVES, P, PACK], BF16, name="d_gd", align_bytes=64)
            nc.vector.scalar_tensor_tensor(
                out=d_gd[u][:, i - firsts[u], 1],
                in0=by_token(banks["thsq", i]),
                scalar=1.0,
                in1=m[i][:],
                op0=ALU.subtract,
                op1=ALU.mult,
            )

        def gate_gradient(i):
            u = unit_of[i]
            nc.vector.tensor_tensor(
                out=d_gd[u][:, i - firsts[u], 0], in0=by_token(banks["th", i]), in1=x2[i][:], op=ALU.mult
            )

        def quantise(u):
            codes[u] = coded.tile([P, SIZES[u] * HALVES * P], U32, name="codes", align_bytes=64)
            scales[u] = coded.tile([P, SIZES[u] * HALVES * P], U8, name="scales", align_bytes=64)
            nc.vector.quantize_mx(
                out=codes[u][:].bitcast(E5M2_X4),
                scales=scales[u][:],
                in_=d_gd[u][:].rearrange("p j g w t -> p (j g w t)"),
            )

        def multiply(u):
            for j in range(SIZES[u]):
                acc[u, j] = psum_two.tile([P, MOVING], F32, name="acc")
                for half in range(HALVES):
                    tokens = slice((j * HALVES + half) * P, (j * HALVES + half + 1) * P)
                    w_cols = slice(half * IN_DIM, half * IN_DIM + MOVING)
                    nc.tensor.matmul_mx(
                        out=acc[u, j][:],
                        lhsT=codes[u][:, tokens].bitcast(E5M2_X4),
                        lhsT_scale=scales[u][:, tokens],
                        rhs=w_codes[:, w_cols].bitcast(E4M3_X4),
                        rhs_scale=w_scales[:, w_cols],
                        start=(half == 0),
                        stop=(half == HALVES - 1),
                    )

        def write_out(u, on_vector):
            if not 0 <= u < units:
                return
            out_sb[u] = store.tile([P, SIZES[u], IN_DIM], F32, name="out_sb")
            for j in range(SIZES[u]):
                if on_vector:
                    nc.vector.tensor_copy(out=out_sb[u][:, j, :], in_=acc[u, j][:, 0:IN_DIM])
                else:
                    nc.scalar.copy(out=out_sb[u][:, j, :], in_=acc[u, j][:, 0:IN_DIM])
            nc.sync.dma_start(out=out_rows[:, firsts[u] : firsts[u] + SIZES[u], :], in_=out_sb[u][:])

        for u in range(PRE_A):
            activations(u)
        sig_log = const.tile([P, PACK], F32)
        nc.scalar.activation(out=sig_log[:], in_=sig_prod[:], func=ACT.Ln)
        ln_bias = const.tile([P, PACK], F32)
        for chunk in range(PACK):
            nc.vector.tensor_scalar(
                out=ln_bias[:, chunk : chunk + 1],
                in0=sig_log[:, chunk : chunk + 1],
                scalar1=neg_inv[:, 0:1],
                scalar2=bias_floor[:, chunk : chunk + 1],
                op0=ALU.mult,
                op1=ALU.add,
            )

        def logarithms(q):
            for chunk in range(PACK):
                logarithm(q, chunk)

        for q in range(BATCHES[0]):
            for chunk in range(PACK):
                logarithm(q, chunk, ("tau_t", "acc")[chunk % 2])

        w_grouped = const.tile([P, HALVES, IN_DIM, PACK], BF16, align_bytes=64)
        for half in range(HALVES):
            nc.vector.tensor_copy(out=w_grouped[:, half], in_=w_raw[:, half].rearrange("p t n -> p n t"))
        w_codes = const.tile([P, 2 * HALVES * IN_DIM], U32, align_bytes=64)
        w_scales = const.tile([P, 2 * HALVES * IN_DIM], U8, align_bytes=64)
        for copy in range(2):
            cols = slice(copy * HALVES * IN_DIM, (copy + 1) * HALVES * IN_DIM)
            nc.vector.quantize_mx(
                out=w_codes[:, cols].bitcast(E4M3_X4),
                scales=w_scales[:, cols],
                in_=w_grouped[:].rearrange("p g n t -> p (g n t)"),
            )

        first_batch = BATCHES[0] * GROUP

        def tile_job(i):
            reciprocals(i)
            if PRE_A <= i < first_batch:
                activations(i)
            if i + EARLY >= first_batch:
                activations(i + EARLY)

        jobs = []
        done = 0
        for b in range(len(BATCHES)):
            jobs.extend((tile_job, i) for i in range(done * GROUP, (done + BATCHES[b]) * GROUP))
            done += BATCHES[b]
            if b + 1 < len(BATCHES):
                jobs.extend((logarithms, q) for q in range(done, done + BATCHES[b + 1]))

        multiplied, copied, hold = [0], [0], [-1]

        def copy_products():
            while copied[0] < multiplied[0]:
                write_out(copied[0], False)
                copied[0] += 1

        def multiply_products(ready, most):
            for count in range(most):
                if multiplied[0] < ready:
                    multiply(multiplied[0])
                    multiplied[0] += 1

        for n in range(-LEAD, TILES):
            group = None
            copy_products()
            if n + LEAD < len(jobs):
                stage, index = jobs[n + LEAD]
                if stage == tile_job and index % GROUP == 0 and taus[0] < GROUPS:
                    load_tau(taus[0])
                    taus[0] += 1
                if stage == logarithms and n >= 0:
                    group = index
                else:
                    stage(index)
            if n == -1:
                for what in ("thsq", "k", "sg", "th"):
                    flip(what, 0)
                shared(0)
                flip("k", 1)
            if n < 0:
                continue
            gate_factor(n)
            flip("sg", n + 1)
            if group is not None:
                logarithm(group, 0, "tau_t")
            if n >= 1:
                quantise(n - 1)
                if group is not None:
                    hold[0] = n + RESUME
                if n > hold[0]:
                    multiply_products(n, CATCH_UP)
            dynamics_gradient(n)
            flip("thsq", n + 1)
            if group is not None:
                logarithm(group, 1, "acc")
            shared(n + 1)
            flip("k", n + 2)
            if group is not None:
                logarithm(group, 2, "tau_t")
            gate_gradient(n)
            flip("th", n + 1)
            if group is not None:
                logarithm(group, 3, "acc")
        copy_products()
        quantise(TILES - 1)
        multiply_products(TILES, CATCH_UP)
        copy_products()
        assert multiplied[0] == TILES
